import numpy as np
import ml_dtypes


def mxq(x, axis, fmt="e4m3"):
    dtype, down = {"e4m3": (ml_dtypes.float8_e4m3fn, 7), "e5m2": (ml_dtypes.float8_e5m2, 14)}[fmt]
    v = np.moveaxis(np.asarray(x, np.float32).astype(ml_dtypes.bfloat16).astype(np.float64), axis, -1)
    blocks = v.reshape(v.shape[:-1] + (-1, 32))
    amax = np.abs(blocks).max(-1, keepdims=True)
    byte = np.maximum(np.where(amax > 0, np.frexp(amax)[1] - 1 + 127, 0) - down, 1)
    scale = np.exp2(byte - 127.0)
    codes = (blocks / scale).astype(np.float32).astype(dtype).astype(np.float64)
    return np.moveaxis((codes * scale).reshape(v.shape), -1, axis)


WIDE = False


def mx_kscale(k):
    if not WIDE:
        return np.ones(k)
    levels = np.array([10, -10, 5, -5, 0])
    if k % 512:
        return np.exp2(np.random.permutation(np.resize(levels, k // 32))).repeat(32)
    a = np.empty((k // 512, 16))
    for p in range(k // 512):
        a[p, :8] = np.random.permutation(np.resize(levels, 8))
        for g in range(8):
            far = levels[np.abs(levels - a[p, g]) >= 10]
            a[p, g + 8] = far[np.random.randint(len(far))]
    return np.exp2(a.ravel()).repeat(32)


BF16 = ml_dtypes.bfloat16


def bf(x):
    return np.asarray(x, np.float32).astype(BF16)


def f64(x):
    return np.asarray(x).astype(np.float64)


E2M1 = np.array([0.0, 0.5, 1.0, 1.5, 2.0, 3.0, 4.0, 6.0, -0.0, -0.5, -1.0, -1.5, -2.0, -3.0, -4.0, -6.0])


def pack_weight(w, fmt):
    k, n = w.shape
    w = f64(bf(w)).reshape(k // 32, 32, n)
    amax = np.abs(w).max(1)
    if fmt == "e4m3":
        byte = np.frexp(amax)[1] - 1 + 127 - 7
    else:
        mant, ex = np.frexp(amax / 6.0)
        byte = np.where(mant > 0.5, ex, ex - 1) + 127
    byte = np.clip(np.where(amax > 0, byte, 1), 1, 254)
    scaled = (w * np.exp2(127.0 - byte)[:, None, :]).reshape(k, n).astype(np.float32)
    by_word = np.ascontiguousarray(scaled.reshape(k // 512, 128, 4, n).transpose(0, 1, 3, 2))
    if fmt == "e4m3":
        words = by_word.astype(ml_dtypes.float8_e4m3fn).view(np.uint8)
    else:
        c = by_word.astype(ml_dtypes.float4_e2m1fn).view(np.uint8) & 0xF
        words = c[..., 0::2] | (c[..., 1::2] << 4)
    return np.ascontiguousarray(words), np.ascontiguousarray(byte.astype(np.uint8).reshape(k // 512, 16, n))


def unpack_weight(words, scales, fmt):
    g, p, n, _ = words.shape
    if fmt == "e4m3":
        vals = np.ascontiguousarray(words).view(ml_dtypes.float8_e4m3fn).astype(np.float64)
    else:
        nib = np.empty((g, p, n, 4), np.uint8)
        nib[..., 0::2] = words & 0xF
        nib[..., 1::2] = words >> 4
        vals = E2M1[nib]
    vals = vals * np.repeat(np.exp2(scales.astype(np.float64) - 127.0), 8, axis=1)[..., None]
    return vals.transpose(0, 1, 3, 2).reshape(g * 512, n)
def pack4(w):
    words, scales = pack_weight(w, "e2m1")
    return words.reshape(words.shape[0], 128, -1), scales


def unpack4(words, scales):
    return unpack_weight(words.reshape(words.shape[0], 128, -1, 2), scales, "e2m1")


B, C, HD, F, G, O = 128, 8, 8, 1024, 512, 128
N = C * HD


def draw0():
    s, t = mx_kscale(F), mx_kscale(G)
    x = bf(np.random.standard_normal((B, C, HD, F)) * s)
    W1g = np.random.standard_normal((G, F)) * 0.7 * np.sqrt(N / F) / s * t[:, None]
    b1g = bf(np.random.standard_normal(G) * 0.2 * t)
    W2g = np.random.standard_normal((O, G)) * 1.5 / np.sqrt(G) / t
    b2g = bf(np.random.standard_normal(O) * 0.2)
    W1g_words, W1g_scales = pack4(W1g.T)
    W2g_words, W2g_scales = pack4(W2g.T)
    return {
        "x": x,
        "W1g_words": W1g_words,
        "W1g_scales": W1g_scales,
        "b1g": b1g,
        "W2g_words": W2g_words,
        "W2g_scales": W2g_scales,
        "b2g": b2g,
    }


def core(x, W1g_words, W1g_scales, b1g, W2g_words, W2g_scales, b2g):
    xn = f64(x).reshape(B * N, F)
    y = mxq(xn, 1, "e4m3") @ unpack4(W1g_words, W1g_scales)
    m1 = np.maximum(y.reshape(B, N, G).sum(1) / N + f64(b1g), 0.0)
    m2 = np.maximum((mxq(m1, 1, "e4m3") @ unpack4(W2g_words, W2g_scales)) + f64(b2g), 0.0)
    return np.broadcast_to(m2[:, None, :], (B, N, O)).copy()


def e4m3fn_bytes(y):
    return np.clip(np.asarray(y, np.float64), -448.0, 448.0).astype(np.float32).astype(ml_dtypes.float8_e4m3fn).view(np.uint8)


def e4m3fn_values(b):
    return np.asarray(b, np.uint8).view(ml_dtypes.float8_e4m3fn).astype(np.float64)


def setup_inputs():
    d = draw0()
    x0 = np.asarray(d['x']).astype(np.float64)
    s = (np.max(np.abs(x0), axis=(0, 1, 2), keepdims=True) / 448.0).astype(np.float32)
    out = {}
    for k, v in d.items():
        if k == 'x':
            out['x_bytes'] = e4m3fn_bytes(x0 / s.astype(np.float64))
            out['x_scale'] = s
        else:
            out[k] = v
    return out


def reference(x_bytes, x_scale, W1g_words, W1g_scales, b1g, W2g_words, W2g_scales, b2g):
    return core(e4m3fn_values(x_bytes) * x_scale.astype(np.float64), W1g_words, W1g_scales, b1g, W2g_words, W2g_scales, b2g)

@@ -1,0 +1,417 @@
+from contextlib import ExitStack
+
+import concourse.mybir as mybir
+from concourse.masks import make_block_diagonal, make_identity
+
+F32 = mybir.dt.float32
+BF16 = mybir.dt.bfloat16
+U8 = mybir.dt.uint8
+I32 = mybir.dt.int32
+U32 = mybir.dt.uint32
+FP8 = mybir.dt.float8_e4m3fn
+E4M3X4 = mybir.dt.float8_e4m3fn_x4
+E2M1X4 = mybir.dt.float4_e2m1fn_x4
+MULT = mybir.AluOpType.mult
+ADD = mybir.AluOpType.add
+MAX = mybir.AluOpType.max
+RELU = mybir.ActivationFunctionType.Relu
+COPY = mybir.ActivationFunctionType.Copy
+
+P = 128
+GRAPHS, NODES, F, G, O = 128, 64, 1024, 512, 128
+FLOPS = 2 * GRAPHS * NODES * F * G + 2 * GRAPHS * G * O
+
+GROUPS = (
+    (16, 4, (1, 1, 2)),
+    (32, 4, (4, 4, 4)),
+    (32, 4, (4, 4, 4)),
+    (32, 4, (4, 4, 4)),
+    (16, 0, (4, 2, 1, 1)),
+)
+LATE_START = (0, 2, 5, 8)
+
+
+def tile_gcn_pa_t_w4_kernel(
+    tc, x_bytes, x_scale, W1g_words, W1g_scales, b1g, W2g_words, W2g_scales, b2g, out
+):
+    nc = tc.nc
+    rows = x_bytes.rearrange("b c h f -> (b c h) f")
+
+    with ExitStack() as ctx:
+        keep = ctx.enter_context(tc.tile_pool(name="keep", bufs=1))
+        stage = ctx.enter_context(tc.tile_pool(name="stage", bufs=3))
+        late = ctx.enter_context(tc.tile_pool(name="late", bufs=2))
+        small = ctx.enter_context(tc.tile_pool(name="small", bufs=2))
+        acc_ps = ctx.enter_context(tc.psum_pool(name="acc_ps", bufs=2))
+        tr_ps = ctx.enter_context(tc.psum_pool(name="tr_ps", bufs=4))
+        ty_ps = ctx.enter_context(tc.psum_pool(name="ty_ps", bufs=2))
+
+        steps = []
+        groups = []
+        close = {}
+        y_of_step = {}
+        b0 = 0
+        for q, (graphs, late_tiles, sizes) in enumerate(GROUPS):
+            view = rows[NODES * b0 : NODES * (b0 + graphs), :].rearrange("(p r) f -> p r f", p=P)
+            groups.append((graphs, b0, view, graphs // 2))
+            j0 = late_tiles
+            for n in sizes:
+                steps.append((q, j0, n))
+                j0 += n
+            close[q] = len(steps) - 1
+            if late_tiles:
+                for k in range(4):
+                    y_of_step.setdefault(LATE_START[q] + k, []).append((q, k))
+                close[q] = max(close[q], LATE_START[q] + 3)
+            b0 += graphs
+        n_steps = len(steps)
+
+        scale_sb = keep.tile([P, 2 * F], F32, name="scale_sb", align_bytes=64)
+        scale_kp = keep.tile([P, 2, 4], F32, name="scale_kp", align_bytes=64)
+        nc.scalar.dma_start(
+            out=scale_sb[:, 0:F],
+            in_=x_scale.rearrange("a b c k -> (a b c k)").partition_broadcast(P),
+        )
+        x_tiles = []
+        for i in range(n_steps):
+            x_sb = keep.tile([P, steps[i][2] * F], U8, name="x_sb%d" % i, align_bytes=64)
+            x_tiles.append(x_sb)
+        y_tiles = {}
+        for q, (graphs, late_tiles, sizes) in enumerate(GROUPS):
+            if late_tiles:
+                y_sb = keep.tile([P, 4 * F], U8, name="y_sb%d" % q, align_bytes=64)
+                y_tiles[q] = y_sb
+
+        def load_x(i):
+            q, j0, n = steps[i]
+            nc.sync.dma_start(
+                out=x_tiles[i][:].rearrange("p (r f) -> p r f", f=F),
+                in_=groups[q][2][:, j0 : j0 + n, :],
+            )
+
+        def load_y(q):
+            nc.sync.dma_start(
+                out=y_tiles[q][:].rearrange("p (r f) -> p r f", f=F), in_=groups[q][2][:, 0:4, :]
+            )
+
+        w1_sb = keep.tile([P, 2, 2 * G], U8, name="w1_sb", align_bytes=64)
+        w1_sc = keep.tile([P, 2, G], U8, name="w1_sc", align_bytes=64)
+        w2_sb = keep.tile([P, 2 * O], U8, name="w2_sb", align_bytes=64)
+        w2_sc = keep.tile([P, O], U8, name="w2_sc", align_bytes=64)
+        b1_row = keep.tile([P, G], BF16, name="b1_row", align_bytes=64)
+        b2_sb = keep.tile([P, O], BF16, name="b2_sb", align_bytes=64)
+        ones64 = keep.tile([P, P], BF16, name="ones64", align_bytes=64)
+        ident = keep.tile([P, P], F32, name="ident", align_bytes=64)
+        same_graph4 = keep.tile([P, P], F32, name="same_graph4", align_bytes=64)
+        same_graph8 = keep.tile([P, P], F32, name="same_graph8", align_bytes=64)
+        same_graph = {32: same_graph4, 16: same_graph8}
+
+        make_identity(nc, ident[:])
+        nc.gpsimd.memset(w1_sc[:].rearrange("p g n -> p (g n)").bitcast(I32), 0)
+        nc.gpsimd.memset(w2_sc[:].bitcast(I32), 0)
+        nc.gpsimd.memset(b1_row[:], 0.0)
+        nc.gpsimd.memset(ones64[:], 64.0)
+        make_block_diagonal(nc, same_graph4[:], 4)
+        make_block_diagonal(nc, same_graph8[:], 8)
+
+        with tc.manual_schedule():
+            load_x(0)
+            load_y(0)
+            for i in range(1, 4):
+                load_x(i)
+            nc.sync.dma_start(
+                out=scale_kp[:], in_=x_scale.rearrange("a b c (g p t) -> p (a b c g) t", p=P, t=4)
+            )
+            for quad in range(4):
+                nc.sync.dma_start(
+                    out=w1_sc[32 * quad : 32 * quad + 4, :, :].rearrange("r g n -> r (g n)").bitcast(I32).rearrange(
+                        "r (g n) -> r g n", g=2
+                    ),
+                    in_=W1g_scales[:, 4 * quad : 4 * quad + 4, :].bitcast(I32).rearrange("g r n -> r g n"),
+                )
+            nc.sync.dma_start(out=w1_sb[:], in_=W1g_words.rearrange("g p n -> p g n"))
+            load_x(4)
+            load_y(1)
+            load_x(5)
+            load_x(6)
+            nc.sync.dma_start(out=w2_sb[:], in_=W2g_words[0])
+            for quad in range(4):
+                nc.sync.dma_start(
+                    out=w2_sc[32 * quad : 32 * quad + 4, :].bitcast(I32),
+                    in_=W2g_scales[0, 4 * quad : 4 * quad + 4, :].bitcast(I32),
+                )
+            nc.sync.dma_start(out=b1_row[0:1, :], in_=b1g.unsqueeze(0))
+            nc.sync.dma_start(out=b2_sb[:], in_=b2g.partition_broadcast(P))
+            load_y(2)
+            load_x(7)
+            load_x(8)
+            load_y(3)
+            for i in range(9, n_steps):
+                load_x(i)
+
+            warm = small.tile([P, 1], F32, name="warm")
+            nc.scalar.activation(out=warm[:], in_=ident[:, 0:1], func=RELU)
+
+            x_bf = {}
+            grouped = {}
+            codes = {}
+            scales = {}
+            acc = {}
+            issued = {}
+
+            def mul(i, part):
+                q, j0, n = steps[i]
+                if part == 0:
+                    xs = stage.tile([P, 4 * F], BF16, name="xs", align_bytes=64)
+                    x_bf[i] = xs
+                wide = 1 if i < 3 else 2
+                for a in range(0, n, wide):
+                    if (a > 0) == (part > 0):
+                        w = min(wide, n - a) * F
+                        cols = slice(a * F, a * F + w)
+                        nc.vector.tensor_tensor(
+                            out=x_bf[i][:, cols], in0=x_tiles[i][:, cols].bitcast(FP8), in1=scale_sb[:, 0:w], op=MULT
+                        )
+
+            def turn(i):
+                q, j0, n = steps[i]
+                words = x_bf[i][:].bitcast(F32)
+                gr = stage.tile([P, 4 * F], BF16, name="gr", align_bytes=64)
+                grouped[i] = gr
+                for j in range(n):
+                    tp = tr_ps.tile([P, 512], F32, name="tp", tag="tp")
+                    for g in range(2):
+                        for u in range(2):
+                            w0 = j * 512 + 256 * g
+                            k0 = (2 * g + u) * P
+                            nc.tensor.transpose(tp[:, k0 : k0 + P], words[:, w0 + u : w0 + 256 : 2], ident[:])
+                    nc.scalar.copy(
+                        out=gr[:, j * F : (j + 1) * F].bitcast(F32).rearrange("p (g r u) -> p g r u", g=2, u=2),
+                        in_=tp[:].rearrange("p (g u r) -> p g r u", g=2, u=2),
+                    )
+
+            def quantize(i):
+                q, j0, n = steps[i]
+                cd = stage.tile([P, F], U32, name="cd", align_bytes=64)
+                sc = stage.tile([P, F], U8, name="sc", align_bytes=64)
+                codes[i] = cd
+                scales[i] = sc
+                for a in range(0, n, 2):
+                    w = min(2, n - a) * F
+                    nc.vector.quantize_mx(
+                        out=cd[:, a * 256 : a * 256 + w // 4].bitcast(E4M3X4),
+                        scales=sc[:, a * 256 : a * 256 + w // 4],
+                        in_=grouped[i][:, a * F : a * F + w],
+                    )
+
+            def layer1(q, cd, sc, g):
+                if q not in acc:
+                    ac = acc_ps.tile([P, G], F32, name="ac")
+                    acc[q] = ac
+                    issued[q] = 0
+                issued[q] += 1
+                nc.tensor.matmul_mx(
+                    out=acc[q][:],
+                    lhsT=cd.bitcast(E4M3X4),
+                    lhsT_scale=sc,
+                    rhs=w1_sb[:, g, :].bitcast(E2M1X4),
+                    rhs_scale=w1_sc[:, g, :],
+                    start=(issued[q] == 1),
+                    stop=(issued[q] == 2 * groups[q][3]),
+                )
+
+            def multiply(i):
+                q, j0, n = steps[i]
+                for j in range(n):
+                    for g in range(2):
+                        c0 = (2 * j + g) * P
+                        layer1(q, codes[i][:, c0 : c0 + P], scales[i][:, c0 : c0 + P], g)
+
+            yb = {}
+            yp = {}
+            yg = {}
+            yc = {}
+
+            def y_widen(q):
+                y_bf = late.tile([P, 4 * F], BF16, name="y_bf", align_bytes=64)
+                yb[q] = y_bf
+                for a in range(2):
+                    cols = slice(a * 2 * F, (a + 1) * 2 * F)
+                    nc.scalar.copy(out=y_bf[:, cols], in_=y_tiles[q][:, cols].bitcast(FP8))
+
+            def y_turn(q, g):
+                words = yb[q][:].bitcast(F32)
+                pairs = late.tile([P, 2, 512, 2], BF16, name="pairs", align_bytes=64)
+                yp[q, g] = pairs
+                for u in range(2):
+                    ty = ty_ps.tile([P, 512], F32, name="ty")
+                    for j in range(4):
+                        w0 = j * 512 + 256 * g
+                        nc.tensor.transpose(
+                            ty[:, j * P : (j + 1) * P], words[:, w0 + u : w0 + 256 : 2], ident[:]
+                        )
+                    for e in range(2):
+                        t = 2 * u + e
+                        nc.scalar.activation(
+                            out=pairs[:, u, :, e],
+                            in_=ty[:].bitcast(BF16).rearrange("p (r e) -> p r e", e=2)[:, :, e],
+                            func=COPY,
+                            scale=scale_kp[:, g, t : t + 1],
+                        )
+
+            def y_interleave(q, g):
+                four = late.tile([P, 512, 4], BF16, name="four", align_bytes=64)
+                yg[q, g] = four
+                nc.vector.tensor_copy(
+                    out=four[:].rearrange("p r k -> p (r k)").bitcast(F32).rearrange("p (r u) -> p r u", u=2),
+                    in_=yp[q, g][:].rearrange("p u r e -> p (u r e)").bitcast(F32).rearrange("p (u r) -> p r u", u=2),
+                )
+
+            def y_quantize(q, g):
+                ycd = late.tile([P, 512], U32, name="ycd", align_bytes=64)
+                ysc = late.tile([P, 512], U8, name="ysc", align_bytes=64)
+                yc[q, g] = (ycd, ysc)
+                nc.vector.quantize_mx(
+                    out=ycd[:].bitcast(E4M3X4),
+                    scales=ysc[:],
+                    in_=yg[q, g][:].rearrange("p r k -> p (r k)"),
+                )
+
+            def y_multiply(q):
+                for g in range(2):
+                    for j in range(4):
+                        ycd, ysc = yc[q, g]
+                        layer1(q, ycd[:, j * P : (j + 1) * P], ysc[:, j * P : (j + 1) * P], g)
+
+            fin = {}
+
+            def fin_copy(q):
+                y = small.tile([P, 4, P], F32, name="y", align_bytes=64)
+                fin["y", q] = y
+                nc.scalar.copy(out=y[:], in_=acc[q][:].rearrange("p (m t) -> p t m", t=4))
+
+            def fin_sum(q):
+                pre = tr_ps.tile([P, 4, P], F32, name="pre", tag="tp")
+                fin["pre", q] = pre
+                for t in range(4):
+                    nc.tensor.matmul(
+                        pre[:, t, :], lhsT=b1_row[:, t:G:4], rhs=ones64[:], start=True, stop=False
+                    )
+                    nc.tensor.matmul(
+                        pre[:, t, :],
+                        lhsT=fin["y", q][:, t, :],
+                        rhs=same_graph[groups[q][0]][:],
+                        start=False,
+                        stop=True,
+                    )
+
+            def fin_relu(q):
+                m1 = small.tile([P, P, 4], BF16, name="m1", align_bytes=64)
+                fin["m1", q] = m1
+                nc.scalar.activation(
+                    out=m1[:], in_=fin["pre", q][:].rearrange("p t n -> p n t"), func=RELU, scale=1.0 / NODES
+                )
+
+            def fin_quantize(q):
+                m1c = small.tile([P, P], U32, name="m1c", align_bytes=64)
+                m1s = small.tile([P, P], U8, name="m1s", align_bytes=64)
+                nc.vector.quantize_mx(
+                    out=m1c[:].bitcast(E4M3X4),
+                    scales=m1s[:],
+                    in_=fin["m1", q][:].rearrange("p n t -> p (n t)"),
+                )
+                fin["m1q", q] = (m1c, m1s)
+
+            def fin_multiply(q):
+                o_ps = tr_ps.tile([P, 512], F32, name="o_ps", tag="tp")
+                fin["o", q] = o_ps
+                m1c, m1s = fin["m1q", q]
+                nc.tensor.matmul_mx(
+                    out=o_ps[:, 0:O],
+                    lhsT=m1c[:].bitcast(E4M3X4),
+                    lhsT_scale=m1s[:],
+                    rhs=w2_sb[:].bitcast(E2M1X4),
+                    rhs_scale=w2_sc[:],
+                    start=True,
+                    stop=True,
+                )
+
+            def fin_store(q):
+                graphs, first, view, tiles = groups[q]
+                tmp = small.tile([P, O], F32, name="tmp", align_bytes=64)
+                nc.vector.tensor_tensor(out=tmp[:], in0=fin["o", q][:, 0:O], in1=b2_sb[:], op=ADD)
+                o_sb = small.tile([P, 4, O], F32, name="o_sb", align_bytes=64)
+                nc.vector.tensor_scalar(
+                    out=o_sb[:], in0=tmp[:].unsqueeze(1).to_broadcast([P, 4, O]), scalar1=0.0, scalar2=None, op0=MAX
+                )
+                reps = P // graphs
+                nodes = NODES // reps
+                dst = out[first : first + graphs].rearrange("b (r n) o -> (b r) (n o)", r=reps)
+                nc.sync.dma_start(
+                    out=dst.rearrange("p (k m) -> p k m", m=4 * O),
+                    in_=o_sb[:].rearrange("p k o -> p (k o)").unsqueeze(1).to_broadcast([P, nodes // 4, 4 * O]),
+                )
+
+            todo = {}
+
+            def at(step, where, fn, q):
+                todo.setdefault((step, where), []).append((fn, q))
+
+            def run(step, where):
+                for fn, q in todo.get((step, where), []):
+                    fn(q)
+
+            for q in range(len(GROUPS) - 1):
+                c = close[q]
+                at(c + 1, "mid", fin_copy, q)
+                at(c + 2, "sum", fin_sum, q)
+                at(c + 2, "mid", fin_relu, q)
+                at(c + 3, "mid", fin_quantize, q)
+                at(c + 4, "sum", fin_multiply, q)
+                at(c + 4, "end", fin_store, q)
+
+            def late_items(i, stage_no):
+                return [q for q, k in y_of_step.get(i, []) if k == stage_no]
+
+            mul(0, 0)
+            mul(1, 0)
+            y_widen(0)
+            turn(0)
+            for i in range(n_steps):
+                for q in late_items(i, 3):
+                    y_interleave(q, 1)
+                for q in late_items(i, 2):
+                    y_interleave(q, 0)
+                if i + 2 < n_steps:
+                    mul(i + 2, 0)
+                if i > 0:
+                    for q in late_items(i, 0):
+                        y_widen(q)
+                for q in late_items(i, 1):
+                    y_turn(q, 0)
+                for q in late_items(i, 2):
+                    y_turn(q, 1)
+                run(i, "sum")
+                if i + 1 < n_steps:
+                    turn(i + 1)
+                run(i, "mid")
+                quantize(i)
+                if i == 0:
+                    nc.scalar.copy(out=scale_sb[:, F : 2 * F], in_=scale_sb[:, 0:F])
+                for q in late_items(i, 2):
+                    y_quantize(q, 0)
+                for q in late_items(i, 3):
+                    y_quantize(q, 1)
+                if i + 2 < n_steps:
+                    mul(i + 2, 1)
+                multiply(i)
+                for q in late_items(i, 3):
+                    y_multiply(q)
+                run(i, "end")
+            q = len(GROUPS) - 1
+            fin_copy(q)
+            fin_sum(q)
+            fin_relu(q)
+            fin_quantize(q)
+            fin_multiply(q)
+            fin_store(q)

@@ -21,14 +21,14 @@ P = 128
 GRAPHS, NODES, F, G, O = 128, 64, 1024, 512, 128
 FLOPS = 2 * GRAPHS * NODES * F * G + 2 * GRAPHS * G * O
 
-GROUPS = (
-    (16, 4, (1, 1, 2)),
-    (32, 4, (4, 4, 4)),
-    (32, 4, (4, 4, 4)),
-    (32, 4, (4, 4, 4)),
-    (16, 0, (4, 2, 1, 1)),
-)
-LATE_START = (0, 2, 5, 8)
+GROUPS = ((16, 4, (1, 1, 2)), (64, 8, (3, 3, 3, 3, 3, 3, 3, 3)), (32, 4, (3, 3, 3, 3)), (16, 0, (1, 2, 2, 3)))
+LATE = ((0, 0, (-1, -1, 0, 1, 2, 2, 3, 3)), (1, 0, (4, 4, 4, 5, 6, 7, 8, 8)), (1, 4, (5, 8, 9, 10, 10, 11, 13, 13)), (2, 0, (9, 9, 12, 12, 13, 14, 15, 15)))
+ORDER = ('sum', 'qz', 'C', 'W', 'turnA', 'end', 'mid', 'E', 'qY', 'mmA', 'mulA', 'mmY')
+FIN = (1, 2, 3, 4, 4)
+VW = 1
+DUM = (0, 2, 0, 3, 0, 0)
+AHEAD = 2
+TAHEAD = 1
 
 
 def tile_gcn_pa_t_w4_kernel(
@@ -39,7 +39,7 @@ def tile_gcn_pa_t_w4_kernel(
 
     with ExitStack() as ctx:
         keep = ctx.enter_context(tc.tile_pool(name="keep", bufs=1))
-        stage = ctx.enter_context(tc.tile_pool(name="stage", bufs=3))
+        stage = ctx.enter_context(tc.tile_pool(name="stage", bufs=5))
         late = ctx.enter_context(tc.tile_pool(name="late", bufs=2))
         small = ctx.enter_context(tc.tile_pool(name="small", bufs=2))
         acc_ps = ctx.enter_context(tc.psum_pool(name="acc_ps", bufs=2))
@@ -49,7 +49,6 @@ def tile_gcn_pa_t_w4_kernel(
         steps = []
         groups = []
         close = {}
-        y_of_step = {}
         b0 = 0
         for q, (graphs, late_tiles, sizes) in enumerate(GROUPS):
             view = rows[NODES * b0 : NODES * (b0 + graphs), :].rearrange("(p r) f -> p r f", p=P)
@@ -59,11 +58,9 @@ def tile_gcn_pa_t_w4_kernel(
                 steps.append((q, j0, n))
                 j0 += n
             close[q] = len(steps) - 1
-            if late_tiles:
-                for k in range(4):
-                    y_of_step.setdefault(LATE_START[q] + k, []).append((q, k))
-                close[q] = max(close[q], LATE_START[q] + 3)
             b0 += graphs
+        for q, j0, when in LATE:
+            close[q] = max(close[q], when[7])
         n_steps = len(steps)
 
         scale_sb = keep.tile([P, 2 * F], F32, name="scale_sb", align_bytes=64)
@@ -72,15 +69,17 @@ def tile_gcn_pa_t_w4_kernel(
             out=scale_sb[:, 0:F],
             in_=x_scale.rearrange("a b c k -> (a b c k)").partition_broadcast(P),
         )
+        nc.scalar.dma_start(
+            out=scale_kp[:], in_=x_scale.rearrange("a b c (g p t) -> p (a b c g) t", p=P, t=4)
+        )
         x_tiles = []
         for i in range(n_steps):
             x_sb = keep.tile([P, steps[i][2] * F], U8, name="x_sb%d" % i, align_bytes=64)
             x_tiles.append(x_sb)
-        y_tiles = {}
-        for q, (graphs, late_tiles, sizes) in enumerate(GROUPS):
-            if late_tiles:
-                y_sb = keep.tile([P, 4 * F], U8, name="y_sb%d" % q, align_bytes=64)
-                y_tiles[q] = y_sb
+        y_tiles = []
+        for k in range(len(LATE)):
+            y_sb = keep.tile([P, 4 * F], U8, name="y_sb%d" % k, align_bytes=64)
+            y_tiles.append(y_sb)
 
         def load_x(i):
             q, j0, n = steps[i]
@@ -89,9 +88,11 @@ def tile_gcn_pa_t_w4_kernel(
                 in_=groups[q][2][:, j0 : j0 + n, :],
             )
 
-        def load_y(q):
+        def load_y(k, half):
+            q, j0, when = LATE[k]
             nc.sync.dma_start(
-                out=y_tiles[q][:].rearrange("p (r f) -> p r f", f=F), in_=groups[q][2][:, 0:4, :]
+                out=y_tiles[k][:, half * 2 * F : (half + 1) * 2 * F].rearrange("p (r f) -> p r f", f=F),
+                in_=groups[q][2][:, j0 + 2 * half : j0 + 2 * half + 2, :],
             )
 
         w1_sb = keep.tile([P, 2, 2 * G], U8, name="w1_sb", align_bytes=64)
@@ -101,27 +102,30 @@ def tile_gcn_pa_t_w4_kernel(
         b1_row = keep.tile([P, G], BF16, name="b1_row", align_bytes=64)
         b2_sb = keep.tile([P, O], BF16, name="b2_sb", align_bytes=64)
         ones64 = keep.tile([P, P], BF16, name="ones64", align_bytes=64)
+        zero = keep.tile([P, 512], BF16, name="zero", align_bytes=64)
+        nc.vector.memset(zero[:], 0.0)
         ident = keep.tile([P, P], F32, name="ident", align_bytes=64)
         same_graph4 = keep.tile([P, P], F32, name="same_graph4", align_bytes=64)
         same_graph8 = keep.tile([P, P], F32, name="same_graph8", align_bytes=64)
-        same_graph = {32: same_graph4, 16: same_graph8}
+        same_graph2 = keep.tile([P, P], F32, name="same_graph2", align_bytes=64)
+        same_graph = {64: same_graph2, 32: same_graph4, 16: same_graph8}
 
-        make_identity(nc, ident[:])
         nc.gpsimd.memset(w1_sc[:].rearrange("p g n -> p (g n)").bitcast(I32), 0)
+        make_identity(nc, ident[:])
         nc.gpsimd.memset(w2_sc[:].bitcast(I32), 0)
         nc.gpsimd.memset(b1_row[:], 0.0)
         nc.gpsimd.memset(ones64[:], 64.0)
         make_block_diagonal(nc, same_graph4[:], 4)
         make_block_diagonal(nc, same_graph8[:], 8)
+        make_block_diagonal(nc, same_graph2[:], 2)
 
         with tc.manual_schedule():
+            load_y(0, 0)
             load_x(0)
-            load_y(0)
-            for i in range(1, 4):
-                load_x(i)
-            nc.sync.dma_start(
-                out=scale_kp[:], in_=x_scale.rearrange("a b c (g p t) -> p (a b c g) t", p=P, t=4)
-            )
+            nc.sync.dma_start(out=w1_sb[:], in_=W1g_words.rearrange("g p n -> p g n"))
+            load_x(1)
+            load_y(0, 1)
+            load_x(2)
             for quad in range(4):
                 nc.sync.dma_start(
                     out=w1_sc[32 * quad : 32 * quad + 4, :, :].rearrange("r g n -> r (g n)").bitcast(I32).rearrange(
@@ -129,25 +133,21 @@ def tile_gcn_pa_t_w4_kernel(
                     ),
                     in_=W1g_scales[:, 4 * quad : 4 * quad + 4, :].bitcast(I32).rearrange("g r n -> r g n"),
                 )
-            nc.sync.dma_start(out=w1_sb[:], in_=W1g_words.rearrange("g p n -> p g n"))
-            load_x(4)
-            load_y(1)
-            load_x(5)
-            load_x(6)
-            nc.sync.dma_start(out=w2_sb[:], in_=W2g_words[0])
-            for quad in range(4):
-                nc.sync.dma_start(
-                    out=w2_sc[32 * quad : 32 * quad + 4, :].bitcast(I32),
-                    in_=W2g_scales[0, 4 * quad : 4 * quad + 4, :].bitcast(I32),
-                )
-            nc.sync.dma_start(out=b1_row[0:1, :], in_=b1g.unsqueeze(0))
-            nc.sync.dma_start(out=b2_sb[:], in_=b2g.partition_broadcast(P))
-            load_y(2)
-            load_x(7)
-            load_x(8)
-            load_y(3)
-            for i in range(9, n_steps):
+            for i in range(3, n_steps):
                 load_x(i)
+                for k in range(1, len(LATE)):
+                    if max(LATE[k][2][0], 3) == i:
+                        load_y(k, 0)
+                        load_y(k, 1)
+                if i == 6:
+                    nc.sync.dma_start(out=b1_row[0:1, :], in_=b1g.unsqueeze(0))
+                    nc.sync.dma_start(out=b2_sb[:], in_=b2g.partition_broadcast(P))
+                    nc.sync.dma_start(out=w2_sb[:], in_=W2g_words[0])
+                    for quad in range(4):
+                        nc.sync.dma_start(
+                            out=w2_sc[32 * quad : 32 * quad + 4, :].bitcast(I32),
+                            in_=W2g_scales[0, 4 * quad : 4 * quad + 4, :].bitcast(I32),
+                        )
 
             warm = small.tile([P, 1], F32, name="warm")
             nc.scalar.activation(out=warm[:], in_=ident[:, 0:1], func=RELU)
@@ -159,19 +159,17 @@ def tile_gcn_pa_t_w4_kernel(
             acc = {}
             issued = {}
 
-            def mul(i, part):
+            def mul(i):
                 q, j0, n = steps[i]
-                if part == 0:
-                    xs = stage.tile([P, 4 * F], BF16, name="xs", align_bytes=64)
-                    x_bf[i] = xs
+                xs = stage.tile([P, 4 * F], BF16, name="xs", align_bytes=64)
+                x_bf[i] = xs
                 wide = 1 if i < 3 else 2
                 for a in range(0, n, wide):
-                    if (a > 0) == (part > 0):
-                        w = min(wide, n - a) * F
-                        cols = slice(a * F, a * F + w)
-                        nc.vector.tensor_tensor(
-                            out=x_bf[i][:, cols], in0=x_tiles[i][:, cols].bitcast(FP8), in1=scale_sb[:, 0:w], op=MULT
-                        )
+                    w = min(wide, n - a) * F
+                    cols = slice(a * F, a * F + w)
+                    nc.vector.tensor_tensor(
+                        out=xs[:, cols], in0=x_tiles[i][:, cols].bitcast(FP8), in1=scale_sb[:, 0:w], op=MULT
+                    )
 
             def turn(i):
                 q, j0, n = steps[i]
@@ -192,16 +190,16 @@ def tile_gcn_pa_t_w4_kernel(
 
             def quantize(i):
                 q, j0, n = steps[i]
-                cd = stage.tile([P, F], U32, name="cd", align_bytes=64)
-                sc = stage.tile([P, F], U8, name="sc", align_bytes=64)
+                cd = stage.tile([P, 1024], U32, name="cd", align_bytes=64)
+                sc = stage.tile([P, 1024], U8, name="sc", align_bytes=64)
                 codes[i] = cd
                 scales[i] = sc
                 for a in range(0, n, 2):
-                    w = min(2, n - a) * F
+                    b = min(n, a + 2)
                     nc.vector.quantize_mx(
-                        out=cd[:, a * 256 : a * 256 + w // 4].bitcast(E4M3X4),
-                        scales=sc[:, a * 256 : a * 256 + w // 4],
-                        in_=grouped[i][:, a * F : a * F + w],
+                        out=cd[:, a * 256 : b * 256].bitcast(E4M3X4),
+                        scales=sc[:, a * 256 : b * 256],
+                        in_=grouped[i][:, a * F : b * F],
                     )
 
             def layer1(q, cd, sc, g):
@@ -232,32 +230,33 @@ def tile_gcn_pa_t_w4_kernel(
             yg = {}
             yc = {}
 
-            def y_widen(q):
-                y_bf = late.tile([P, 4 * F], BF16, name="y_bf", align_bytes=64)
-                yb[q] = y_bf
-                for a in range(2):
-                    cols = slice(a * 2 * F, (a + 1) * 2 * F)
-                    nc.scalar.copy(out=y_bf[:, cols], in_=y_tiles[q][:, cols].bitcast(FP8))
+            def y_widen(k, half):
+                if half == 0:
+                    y_bf = late.tile([P, 4 * F], BF16, name="y_bf", align_bytes=64)
+                    yb[k] = y_bf
+                cols = slice(half * 2 * F, (half + 1) * 2 * F)
+                if VW and k == 0 and half == 0:
+                    nc.vector.tensor_copy(out=yb[k][:, cols], in_=y_tiles[k][:, cols].bitcast(FP8))
+                else:
+                    nc.scalar.copy(out=yb[k][:, cols], in_=y_tiles[k][:, cols].bitcast(FP8))
 
-            def y_turn(q, g):
-                words = yb[q][:].bitcast(F32)
-                pairs = late.tile([P, 2, 512, 2], BF16, name="pairs", align_bytes=64)
-                yp[q, g] = pairs
-                for u in range(2):
-                    ty = ty_ps.tile([P, 512], F32, name="ty")
-                    for j in range(4):
-                        w0 = j * 512 + 256 * g
-                        nc.tensor.transpose(
-                            ty[:, j * P : (j + 1) * P], words[:, w0 + u : w0 + 256 : 2], ident[:]
-                        )
-                    for e in range(2):
-                        t = 2 * u + e
-                        nc.scalar.activation(
-                            out=pairs[:, u, :, e],
-                            in_=ty[:].bitcast(BF16).rearrange("p (r e) -> p r e", e=2)[:, :, e],
-                            func=COPY,
-                            scale=scale_kp[:, g, t : t + 1],
-                        )
+            def y_turn(k, g, u):
+                words = yb[k][:].bitcast(F32)
+                if u == 0:
+                    pairs = late.tile([P, 2, 512, 2], BF16, name="pairs", align_bytes=64)
+                    yp[k, g] = pairs
+                ty = ty_ps.tile([P, 512], F32, name="ty")
+                for j in range(4):
+                    w0 = j * 512 + 256 * g
+                    nc.tensor.transpose(ty[:, j * P : (j + 1) * P], words[:, w0 + u : w0 + 256 : 2], ident[:])
+                for e in range(2):
+                    t = 2 * u + e
+                    nc.scalar.activation(
+                        out=yp[k, g][:, u, :, e],
+                        in_=ty[:].bitcast(BF16).rearrange("p (r e) -> p r e", e=2)[:, :, e],
+                        func=COPY,
+                        scale=scale_kp[:, g, t : t + 1],
+                    )
 
             def y_interleave(q, g):
                 four = late.tile([P, 512, 4], BF16, name="four", align_bytes=64)
@@ -277,11 +276,10 @@ def tile_gcn_pa_t_w4_kernel(
                     in_=yg[q, g][:].rearrange("p r k -> p (r k)"),
                 )
 
-            def y_multiply(q):
-                for g in range(2):
-                    for j in range(4):
-                        ycd, ysc = yc[q, g]
-                        layer1(q, ycd[:, j * P : (j + 1) * P], ysc[:, j * P : (j + 1) * P], g)
+            def y_multiply(k, g):
+                ycd, ysc = yc[k, g]
+                for j in range(4):
+                    layer1(LATE[k][0], ycd[:, j * P : (j + 1) * P], ysc[:, j * P : (j + 1) * P], g)
 
             fin = {}
 
@@ -363,51 +361,68 @@ def tile_gcn_pa_t_w4_kernel(
 
             for q in range(len(GROUPS) - 1):
                 c = close[q]
-                at(c + 1, "mid", fin_copy, q)
-                at(c + 2, "sum", fin_sum, q)
-                at(c + 2, "mid", fin_relu, q)
-                at(c + 3, "mid", fin_quantize, q)
-                at(c + 4, "sum", fin_multiply, q)
-                at(c + 4, "end", fin_store, q)
+                at(c + FIN[0], "mid", fin_copy, q)
+                at(c + FIN[1], "sum", fin_sum, q)
+                at(c + FIN[1], "mid", fin_relu, q)
+                at(c + FIN[2], "mid", fin_quantize, q)
+                at(c + FIN[3], "sum", fin_multiply, q)
+                at(c + FIN[4], "end", fin_store, q)
 
-            def late_items(i, stage_no):
-                return [q for q, k in y_of_step.get(i, []) if k == stage_no]
+            def late_items(i, first_stage, n_stages):
+                return [
+                    (k, s) for s in range(n_stages) for k in range(len(LATE)) if LATE[k][2][first_stage + s] == i
+                ]
 
-            mul(0, 0)
-            mul(1, 0)
-            y_widen(0)
-            turn(0)
+            def warm_up(k):
+                if k < len(DUM) and DUM[k]:
+                    du = tr_ps.tile([P, 512], F32, name="du", tag="tp")
+                    for n in range(DUM[k]):
+                        nc.tensor.matmul(du[:], lhsT=zero[:, 0:P], rhs=zero[:], start=True, stop=True)
+
+            warm_up(0)
+            for k, half in late_items(-1, 0, 2):
+                y_widen(k, half)
+            for i in range(AHEAD):
+                mul(i)
+            for i in range(TAHEAD):
+                turn(i)
             for i in range(n_steps):
-                for q in late_items(i, 3):
-                    y_interleave(q, 1)
-                for q in late_items(i, 2):
-                    y_interleave(q, 0)
-                if i + 2 < n_steps:
-                    mul(i + 2, 0)
-                if i > 0:
-                    for q in late_items(i, 0):
-                        y_widen(q)
-                for q in late_items(i, 1):
-                    y_turn(q, 0)
-                for q in late_items(i, 2):
-                    y_turn(q, 1)
-                run(i, "sum")
-                if i + 1 < n_steps:
-                    turn(i + 1)
-                run(i, "mid")
-                quantize(i)
-                if i == 0:
-                    nc.scalar.copy(out=scale_sb[:, F : 2 * F], in_=scale_sb[:, 0:F])
-                for q in late_items(i, 2):
-                    y_quantize(q, 0)
-                for q in late_items(i, 3):
-                    y_quantize(q, 1)
-                if i + 2 < n_steps:
-                    mul(i + 2, 1)
-                multiply(i)
-                for q in late_items(i, 3):
-                    y_multiply(q)
-                run(i, "end")
+                warm_up(i + 1)
+                for what in ORDER:
+                    if what == "C":
+                        for k, g in late_items(i, 6, 2):
+                            y_interleave(k, g)
+                    elif what == "mulA" and i + AHEAD < n_steps:
+                        mul(i + AHEAD)
+                    elif what == "W":
+                        for k, half in late_items(i, 0, 2):
+                            y_widen(k, half)
+                    elif what == "E":
+                        for k, gu in late_items(i, 2, 4):
+                            y_turn(k, gu // 2, gu % 2)
+                    elif what == "sum":
+                        run(i, "sum")
+                    elif what == "turnA" and i + TAHEAD < n_steps:
+                        turn(i + TAHEAD)
+                    elif what == "mid":
+                        run(i, "mid")
+                    elif what == "qz":
+                        quantize(i)
+                        if i == 0:
+                            nc.scalar.copy(out=scale_sb[:, F : 2 * F], in_=scale_sb[:, 0:F])
+                    elif what == "qY":
+                        for k, g in late_items(i, 6, 2):
+                            y_quantize(k, g)
+                    elif what == "mmA":
+                        multiply(i)
+                    elif what == "mmY":
+                        for k, g in late_items(i, 6, 2):
+                            y_multiply(k, g)
+                    elif what == "end":
+                        run(i, "end")
+            for i in range(n_steps, n_steps + 10):
+                for where in ("sum", "mid", "end"):
+                    run(i, where)
             q = len(GROUPS) - 1
             fin_copy(q)
             fin_sum(q)

@@ -21,14 +21,21 @@ P = 128
 GRAPHS, NODES, F, G, O = 128, 64, 1024, 512, 128
 FLOPS = 2 * GRAPHS * NODES * F * G + 2 * GRAPHS * G * O
 
-GROUPS = ((16, 4, (1, 1, 2)), (64, 8, (3, 3, 3, 3, 3, 3, 3, 3)), (32, 4, (3, 3, 3, 3)), (16, 0, (1, 2, 2, 3)))
-LATE = ((0, 0, (-1, -1, 0, 1, 2, 2, 3, 3)), (1, 0, (4, 4, 4, 5, 6, 7, 8, 8)), (1, 4, (5, 8, 9, 10, 10, 11, 13, 13)), (2, 0, (9, 9, 12, 12, 13, 14, 15, 15)))
-ORDER = ('sum', 'qz', 'C', 'W', 'turnA', 'end', 'mid', 'E', 'qY', 'mmA', 'mulA', 'mmY')
-FIN = (1, 2, 3, 4, 4)
-VW = 1
-DUM = (0, 2, 0, 3, 0, 0)
-AHEAD = 2
-TAHEAD = 1
+GROUPS = ((16, 4, (1, 1, 1, 1)), (64, 12, (2, 2, 2, 2, 2, 2, 2, 2, 2, 2)), (32, 4, (3, 3, 2, 2, 2)), (16, 0, (1, 3, 2, 2)))
+LATE = ((0, 0, (-1, 0, 1, 2, 3, 5, 5, 11)), (1, 0, (1, 4, 5, 6, 8, 8, 8, 13)), (1, 4, (8, 8, 9, 9, 10, 10, 12, 12)), (1, 8, (10, 11, 12, 12, 13, 13, 15, 15)), (2, 0, (13, 14, 15, 15, 16, 16, 18, 18)))
+ORDER = ('sum', 'mid', 'du', 'qz', 'C', 'W', 'qY', 'mulA', 'turnA', 'mmA', 'E', 'end', 'mmY')
+FIN = (1, 2, 4, 5, 5)
+VW = 0
+DUP = 4
+WV = ((2, 1),)
+XV = (1, 3, 18, 19, 22, 27, 28, 30, 41)
+DUM = (6, 2, 0, 1, 0, 0, 0, 0, 0, 0, 0, 2)
+AHEAD = 3
+TAHEAD = 2
+SB = 4
+OUT = 2
+HEAD = ('y0', 's01', 'x0', 'x1', 'y1', 's12', 'x2', 'w1', 'q', 'kp')
+LB = 4
 
 
 def tile_gcn_pa_t_w4_kernel(
@@ -39,8 +46,8 @@ def tile_gcn_pa_t_w4_kernel(
 
     with ExitStack() as ctx:
         keep = ctx.enter_context(tc.tile_pool(name="keep", bufs=1))
-        stage = ctx.enter_context(tc.tile_pool(name="stage", bufs=5))
-        late = ctx.enter_context(tc.tile_pool(name="late", bufs=2))
+        stage = ctx.enter_context(tc.tile_pool(name="stage", bufs=SB))
+        late = ctx.enter_context(tc.tile_pool(name="late", bufs=LB))
         small = ctx.enter_context(tc.tile_pool(name="small", bufs=2))
         acc_ps = ctx.enter_context(tc.psum_pool(name="acc_ps", bufs=2))
         tr_ps = ctx.enter_context(tc.psum_pool(name="tr_ps", bufs=4))
@@ -62,16 +69,10 @@ def tile_gcn_pa_t_w4_kernel(
         for q, j0, when in LATE:
             close[q] = max(close[q], when[7])
         n_steps = len(steps)
+        widest = max(n for q, j0, n in steps)
 
         scale_sb = keep.tile([P, 2 * F], F32, name="scale_sb", align_bytes=64)
         scale_kp = keep.tile([P, 2, 4], F32, name="scale_kp", align_bytes=64)
-        nc.scalar.dma_start(
-            out=scale_sb[:, 0:F],
-            in_=x_scale.rearrange("a b c k -> (a b c k)").partition_broadcast(P),
-        )
-        nc.scalar.dma_start(
-            out=scale_kp[:], in_=x_scale.rearrange("a b c (g p t) -> p (a b c g) t", p=P, t=4)
-        )
         x_tiles = []
         for i in range(n_steps):
             x_sb = keep.tile([P, steps[i][2] * F], U8, name="x_sb%d" % i, align_bytes=64)
@@ -109,6 +110,10 @@ def tile_gcn_pa_t_w4_kernel(
         same_graph8 = keep.tile([P, P], F32, name="same_graph8", align_bytes=64)
         same_graph2 = keep.tile([P, P], F32, name="same_graph2", align_bytes=64)
         same_graph = {64: same_graph2, 32: same_graph4, 16: same_graph8}
+        members = {}
+        for graphs in (64, 32, 16):
+            pick = keep.tile([P, graphs], F32, name="pick%d" % graphs, align_bytes=64)
+            members[graphs] = pick
 
         nc.gpsimd.memset(w1_sc[:].rearrange("p g n -> p (g n)").bitcast(I32), 0)
         make_identity(nc, ident[:])
@@ -118,28 +123,41 @@ def tile_gcn_pa_t_w4_kernel(
         make_block_diagonal(nc, same_graph4[:], 4)
         make_block_diagonal(nc, same_graph8[:], 8)
         make_block_diagonal(nc, same_graph2[:], 2)
+        for graphs in (64, 32, 16):
+            nc.gpsimd.tensor_copy(out=members[graphs][:], in_=same_graph[graphs][:, 0 : P : P // graphs])
 
         with tc.manual_schedule():
-            load_y(0, 0)
-            load_x(0)
-            nc.sync.dma_start(out=w1_sb[:], in_=W1g_words.rearrange("g p n -> p g n"))
-            load_x(1)
-            load_y(0, 1)
-            load_x(2)
-            for quad in range(4):
-                nc.sync.dma_start(
-                    out=w1_sc[32 * quad : 32 * quad + 4, :, :].rearrange("r g n -> r (g n)").bitcast(I32).rearrange(
-                        "r (g n) -> r g n", g=2
-                    ),
-                    in_=W1g_scales[:, 4 * quad : 4 * quad + 4, :].bitcast(I32).rearrange("g r n -> r g n"),
-                )
+            scale_row = x_scale.rearrange("a b c k -> (a b c k)")
+            for what in HEAD:
+                if what[0] == "s":
+                    lo = int(what[1]) * F // 2
+                    hi = int(what[2]) * F // 2
+                    nc.scalar.dma_start(out=scale_sb[:, lo:hi], in_=scale_row[lo:hi].partition_broadcast(P))
+                elif what == "kp":
+                    nc.scalar.dma_start(
+                        out=scale_kp[:], in_=x_scale.rearrange("a b c (g p t) -> p (a b c g) t", p=P, t=4)
+                    )
+                elif what[0] == "x":
+                    load_x(int(what[1]))
+                elif what[0] == "y":
+                    load_y(0, int(what[1]))
+                elif what == "w1":
+                    nc.sync.dma_start(out=w1_sb[:], in_=W1g_words.rearrange("g p n -> p g n"))
+                else:
+                    for quad in range(4):
+                        nc.sync.dma_start(
+                            out=w1_sc[32 * quad : 32 * quad + 4, :, :].rearrange("r g n -> r (g n)").bitcast(I32).rearrange(
+                                "r (g n) -> r g n", g=2
+                            ),
+                            in_=W1g_scales[:, 4 * quad : 4 * quad + 4, :].bitcast(I32).rearrange("g r n -> r g n"),
+                        )
             for i in range(3, n_steps):
                 load_x(i)
                 for k in range(1, len(LATE)):
                     if max(LATE[k][2][0], 3) == i:
                         load_y(k, 0)
                         load_y(k, 1)
-                if i == 6:
+                if i == 8:
                     nc.sync.dma_start(out=b1_row[0:1, :], in_=b1g.unsqueeze(0))
                     nc.sync.dma_start(out=b2_sb[:], in_=b2g.partition_broadcast(P))
                     nc.sync.dma_start(out=w2_sb[:], in_=W2g_words[0])
@@ -161,20 +179,26 @@ def tile_gcn_pa_t_w4_kernel(
 
             def mul(i):
                 q, j0, n = steps[i]
-                xs = stage.tile([P, 4 * F], BF16, name="xs", align_bytes=64)
+                xs = stage.tile([P, widest * F], BF16, name="xs", align_bytes=64)
                 x_bf[i] = xs
-                wide = 1 if i < 3 else 2
-                for a in range(0, n, wide):
-                    w = min(wide, n - a) * F
-                    cols = slice(a * F, a * F + w)
+                wide = 1 if i <= DUP + AHEAD else 2
+                piece = F // 2 if i == 0 and "s01" in HEAD else wide * F
+                for c0 in range(0, n * F, piece):
+                    w = min(piece, n * F - c0)
+                    k0 = c0 % F
                     nc.vector.tensor_tensor(
-                        out=xs[:, cols], in0=x_tiles[i][:, cols].bitcast(FP8), in1=scale_sb[:, 0:w], op=MULT
+                        out=xs[:, c0 : c0 + w],
+                        in0=x_tiles[i][:, c0 : c0 + w].bitcast(FP8),
+                        in1=scale_sb[:, k0 : k0 + w],
+                        op=MULT,
                     )
+
+            tile_no = [0]
 
             def turn(i):
                 q, j0, n = steps[i]
                 words = x_bf[i][:].bitcast(F32)
-                gr = stage.tile([P, 4 * F], BF16, name="gr", align_bytes=64)
+                gr = stage.tile([P, widest * F], BF16, name="gr", align_bytes=64)
                 grouped[i] = gr
                 for j in range(n):
                     tp = tr_ps.tile([P, 512], F32, name="tp", tag="tp")
@@ -183,15 +207,18 @@ def tile_gcn_pa_t_w4_kernel(
                             w0 = j * 512 + 256 * g
                             k0 = (2 * g + u) * P
                             nc.tensor.transpose(tp[:, k0 : k0 + P], words[:, w0 + u : w0 + 256 : 2], ident[:])
-                    nc.scalar.copy(
-                        out=gr[:, j * F : (j + 1) * F].bitcast(F32).rearrange("p (g r u) -> p g r u", g=2, u=2),
-                        in_=tp[:].rearrange("p (g u r) -> p g r u", g=2, u=2),
-                    )
+                    out_words = gr[:, j * F : (j + 1) * F].bitcast(F32).rearrange("p (g r u) -> p g r u", g=2, u=2)
+                    in_words = tp[:].rearrange("p (g u r) -> p g r u", g=2, u=2)
+                    if tile_no[0] in XV:
+                        nc.vector.tensor_copy(out=out_words, in_=in_words)
+                    else:
+                        nc.scalar.copy(out=out_words, in_=in_words)
+                    tile_no[0] += 1
 
             def quantize(i):
                 q, j0, n = steps[i]
-                cd = stage.tile([P, 1024], U32, name="cd", align_bytes=64)
-                sc = stage.tile([P, 1024], U8, name="sc", align_bytes=64)
+                cd = stage.tile([P, widest * 256], U32, name="cd", align_bytes=64)
+                sc = stage.tile([P, widest * 256], U8, name="sc", align_bytes=64)
                 codes[i] = cd
                 scales[i] = sc
                 for a in range(0, n, 2):
@@ -235,7 +262,7 @@ def tile_gcn_pa_t_w4_kernel(
                     y_bf = late.tile([P, 4 * F], BF16, name="y_bf", align_bytes=64)
                     yb[k] = y_bf
                 cols = slice(half * 2 * F, (half + 1) * 2 * F)
-                if VW and k == 0 and half == 0:
+                if (k, half) in WV:
                     nc.vector.tensor_copy(out=yb[k][:, cols], in_=y_tiles[k][:, cols].bitcast(FP8))
                 else:
                     nc.scalar.copy(out=yb[k][:, cols], in_=y_tiles[k][:, cols].bitcast(FP8))
@@ -289,25 +316,29 @@ def tile_gcn_pa_t_w4_kernel(
                 nc.scalar.copy(out=y[:], in_=acc[q][:].rearrange("p (m t) -> p t m", t=4))
 
             def fin_sum(q):
-                pre = tr_ps.tile([P, 4, P], F32, name="pre", tag="tp")
+                graphs = groups[q][0]
+                pre = tr_ps.tile([P, 512], F32, name="pre", tag="tp")
                 fin["pre", q] = pre
                 for t in range(4):
+                    cols = slice(t * graphs, (t + 1) * graphs)
                     nc.tensor.matmul(
-                        pre[:, t, :], lhsT=b1_row[:, t:G:4], rhs=ones64[:], start=True, stop=False
+                        pre[:, cols], lhsT=b1_row[:, t:G:4], rhs=ones64[:, 0:graphs], start=True, stop=False
                     )
                     nc.tensor.matmul(
-                        pre[:, t, :],
-                        lhsT=fin["y", q][:, t, :],
-                        rhs=same_graph[groups[q][0]][:],
-                        start=False,
-                        stop=True,
+                        pre[:, cols], lhsT=fin["y", q][:, t, :], rhs=members[graphs][:], start=False, stop=True
                     )
 
             def fin_relu(q):
+                graphs = groups[q][0]
+                reps = P // graphs
                 m1 = small.tile([P, P, 4], BF16, name="m1", align_bytes=64)
                 fin["m1", q] = m1
+                sums = fin["pre", q][:, 0 : 4 * graphs].rearrange("p (t b) -> p b t", t=4)
                 nc.scalar.activation(
-                    out=m1[:], in_=fin["pre", q][:].rearrange("p t n -> p n t"), func=RELU, scale=1.0 / NODES
+                    out=m1[:].rearrange("p (b r) t -> p b r t", r=reps),
+                    in_=sums.unsqueeze(2).to_broadcast([P, graphs, reps, 4]),
+                    func=RELU,
+                    scale=1.0 / NODES,
                 )
 
             def fin_quantize(q):
@@ -338,17 +369,28 @@ def tile_gcn_pa_t_w4_kernel(
                 graphs, first, view, tiles = groups[q]
                 tmp = small.tile([P, O], F32, name="tmp", align_bytes=64)
                 nc.vector.tensor_tensor(out=tmp[:], in0=fin["o", q][:, 0:O], in1=b2_sb[:], op=ADD)
-                o_sb = small.tile([P, 4, O], F32, name="o_sb", align_bytes=64)
-                nc.vector.tensor_scalar(
-                    out=o_sb[:], in0=tmp[:].unsqueeze(1).to_broadcast([P, 4, O]), scalar1=0.0, scalar2=None, op0=MAX
-                )
                 reps = P // graphs
                 nodes = NODES // reps
                 dst = out[first : first + graphs].rearrange("b (r n) o -> (b r) (n o)", r=reps)
-                nc.sync.dma_start(
-                    out=dst.rearrange("p (k m) -> p k m", m=4 * O),
-                    in_=o_sb[:].rearrange("p k o -> p (k o)").unsqueeze(1).to_broadcast([P, nodes // 4, 4 * O]),
-                )
+                if q == len(GROUPS) - 1 or OUT == 0:
+                    o_sb = small.tile([P, 4, O], F32, name="o_sb", align_bytes=64)
+                    nc.vector.tensor_scalar(
+                        out=o_sb[:], in0=tmp[:].unsqueeze(1).to_broadcast([P, 4, O]), scalar1=0.0, scalar2=None, op0=MAX
+                    )
+                    nc.sync.dma_start(
+                        out=dst.rearrange("p (k m) -> p k m", m=4 * O),
+                        in_=o_sb[:].rearrange("p k o -> p (k o)").unsqueeze(1).to_broadcast([P, nodes // 4, 4 * O]),
+                    )
+                else:
+                    o_row = small.tile([P, O], F32, name="o_row", align_bytes=64)
+                    if OUT == 1:
+                        nc.scalar.activation(out=o_row[:], in_=tmp[:], func=RELU)
+                    else:
+                        nc.vector.tensor_scalar(out=o_row[:], in0=tmp[:], scalar1=0.0, scalar2=None, op0=MAX)
+                    nc.sync.dma_start(
+                        out=dst.rearrange("p (k m) -> p k m", m=O),
+                        in_=o_row[:].unsqueeze(1).to_broadcast([P, nodes, O]),
+                    )
 
             todo = {}
 
@@ -387,8 +429,9 @@ def tile_gcn_pa_t_w4_kernel(
             for i in range(TAHEAD):
                 turn(i)
             for i in range(n_steps):
-                warm_up(i + 1)
                 for what in ORDER:
+                    if what == "du":
+                        warm_up(i + 1)
                     if what == "C":
                         for k, g in late_items(i, 6, 2):
                             y_interleave(k, g)
@@ -408,7 +451,7 @@ def tile_gcn_pa_t_w4_kernel(
                         run(i, "mid")
                     elif what == "qz":
                         quantize(i)
-                        if i == 0:
+                        if i == DUP:
                             nc.scalar.copy(out=scale_sb[:, F : 2 * F], in_=scale_sb[:, 0:F])
                     elif what == "qY":
                         for k, g in late_items(i, 6, 2):

from contextlib import ExitStack

import concourse.mybir as mybir
from concourse.masks import make_block_diagonal, make_identity

F32 = mybir.dt.float32
BF16 = mybir.dt.bfloat16
U8 = mybir.dt.uint8
I32 = mybir.dt.int32
U32 = mybir.dt.uint32
FP8 = mybir.dt.float8_e4m3fn
E4M3X4 = mybir.dt.float8_e4m3fn_x4
E2M1X4 = mybir.dt.float4_e2m1fn_x4
MULT = mybir.AluOpType.mult
ADD = mybir.AluOpType.add
MAX = mybir.AluOpType.max
RELU = mybir.ActivationFunctionType.Relu
COPY = mybir.ActivationFunctionType.Copy

P = 128
GRAPHS, NODES, F, G, O = 128, 64, 1024, 512, 128
FLOPS = 2 * GRAPHS * NODES * F * G + 2 * GRAPHS * G * O

GROUPS = ((16, 4, (1, 1, 1, 1)), (64, 12, (2, 2, 2, 2, 2, 2, 2, 2, 2, 2)), (32, 4, (3, 3, 2, 2, 2)), (16, 0, (1, 3, 2, 2)))
LATE = ((0, 0, (-1, 0, 1, 2, 3, 5, 5, 11)), (1, 0, (1, 4, 5, 6, 8, 8, 8, 13)), (1, 4, (8, 8, 9, 9, 10, 10, 12, 12)), (1, 8, (10, 11, 12, 12, 13, 13, 15, 15)), (2, 0, (13, 14, 15, 15, 16, 16, 18, 18)))
ORDER = ('sum', 'mid', 'du', 'qz', 'C', 'W', 'qY', 'mulA', 'turnA', 'mmA', 'E', 'end', 'mmY')
FIN = (1, 2, 4, 5, 5)
VW = 0
DUP = 4
WV = ((2, 1),)
XV = (1, 3, 18, 19, 22, 27, 28, 30, 41)
DUM = (6, 2, 0, 1, 0, 0, 0, 0, 0, 0, 0, 2)
AHEAD = 3
TAHEAD = 2
SB = 4
OUT = 2
HEAD = ('y0', 's01', 'x0', 'x1', 'y1', 's12', 'x2', 'w1', 'q', 'kp')
LB = 4


def tile_gcn_pa_t_w4_kernel(
    tc, x_bytes, x_scale, W1g_words, W1g_scales, b1g, W2g_words, W2g_scales, b2g, out
):
    nc = tc.nc
    rows = x_bytes.rearrange("b c h f -> (b c h) f")

    with ExitStack() as ctx:
        keep = ctx.enter_context(tc.tile_pool(name="keep", bufs=1))
        stage = ctx.enter_context(tc.tile_pool(name="stage", bufs=SB))
        late = ctx.enter_context(tc.tile_pool(name="late", bufs=LB))
        small = ctx.enter_context(tc.tile_pool(name="small", bufs=2))
        acc_ps = ctx.enter_context(tc.psum_pool(name="acc_ps", bufs=2))
        tr_ps = ctx.enter_context(tc.psum_pool(name="tr_ps", bufs=4))
        ty_ps = ctx.enter_context(tc.psum_pool(name="ty_ps", bufs=2))

        steps = []
        groups = []
        close = {}
        b0 = 0
        for q, (graphs, late_tiles, sizes) in enumerate(GROUPS):
            view = rows[NODES * b0 : NODES * (b0 + graphs), :].rearrange("(p r) f -> p r f", p=P)
            groups.append((graphs, b0, view, graphs // 2))
            j0 = late_tiles
            for n in sizes:
                steps.append((q, j0, n))
                j0 += n
            close[q] = len(steps) - 1
            b0 += graphs
        for q, j0, when in LATE:
            close[q] = max(close[q], when[7])
        n_steps = len(steps)
        widest = max(n for q, j0, n in steps)

        scale_sb = keep.tile([P, 2 * F], F32, name="scale_sb", align_bytes=64)
        scale_kp = keep.tile([P, 2, 4], F32, name="scale_kp", align_bytes=64)
        x_tiles = []
        for i in range(n_steps):
            x_sb = keep.tile([P, steps[i][2] * F], U8, name="x_sb%d" % i, align_bytes=64)
            x_tiles.append(x_sb)
        y_tiles = []
        for k in range(len(LATE)):
            y_sb = keep.tile([P, 4 * F], U8, name="y_sb%d" % k, align_bytes=64)
            y_tiles.append(y_sb)

        def load_x(i):
            q, j0, n = steps[i]
            nc.sync.dma_start(
                out=x_tiles[i][:].rearrange("p (r f) -> p r f", f=F),
                in_=groups[q][2][:, j0 : j0 + n, :],
            )

        def load_y(k, half):
            q, j0, when = LATE[k]
            nc.sync.dma_start(
                out=y_tiles[k][:, half * 2 * F : (half + 1) * 2 * F].rearrange("p (r f) -> p r f", f=F),
                in_=groups[q][2][:, j0 + 2 * half : j0 + 2 * half + 2, :],
            )

        w1_sb = keep.tile([P, 2, 2 * G], U8, name="w1_sb", align_bytes=64)
        w1_sc = keep.tile([P, 2, G], U8, name="w1_sc", align_bytes=64)
        w2_sb = keep.tile([P, 2 * O], U8, name="w2_sb", align_bytes=64)
        w2_sc = keep.tile([P, O], U8, name="w2_sc", align_bytes=64)
        b1_row = keep.tile([P, G], BF16, name="b1_row", align_bytes=64)
        b2_sb = keep.tile([P, O], BF16, name="b2_sb", align_bytes=64)
        ones64 = keep.tile([P, P], BF16, name="ones64", align_bytes=64)
        zero = keep.tile([P, 512], BF16, name="zero", align_bytes=64)
        nc.vector.memset(zero[:], 0.0)
        ident = keep.tile([P, P], F32, name="ident", align_bytes=64)
        same_graph4 = keep.tile([P, P], F32, name="same_graph4", align_bytes=64)
        same_graph8 = keep.tile([P, P], F32, name="same_graph8", align_bytes=64)
        same_graph2 = keep.tile([P, P], F32, name="same_graph2", align_bytes=64)
        same_graph = {64: same_graph2, 32: same_graph4, 16: same_graph8}
        members = {}
        for graphs in (64, 32, 16):
            pick = keep.tile([P, graphs], F32, name="pick%d" % graphs, align_bytes=64)
            members[graphs] = pick

        nc.gpsimd.memset(w1_sc[:].rearrange("p g n -> p (g n)").bitcast(I32), 0)
        make_identity(nc, ident[:])
        nc.gpsimd.memset(w2_sc[:].bitcast(I32), 0)
        nc.gpsimd.memset(b1_row[:], 0.0)
        nc.gpsimd.memset(ones64[:], 64.0)
        make_block_diagonal(nc, same_graph4[:], 4)
        make_block_diagonal(nc, same_graph8[:], 8)
        make_block_diagonal(nc, same_graph2[:], 2)
        for graphs in (64, 32, 16):
            nc.gpsimd.tensor_copy(out=members[graphs][:], in_=same_graph[graphs][:, 0 : P : P // graphs])

        with tc.manual_schedule():
            scale_row = x_scale.rearrange("a b c k -> (a b c k)")
            for what in HEAD:
                if what[0] == "s":
                    lo = int(what[1]) * F // 2
                    hi = int(what[2]) * F // 2
                    nc.scalar.dma_start(out=scale_sb[:, lo:hi], in_=scale_row[lo:hi].partition_broadcast(P))
                elif what == "kp":
                    nc.scalar.dma_start(
                        out=scale_kp[:], in_=x_scale.rearrange("a b c (g p t) -> p (a b c g) t", p=P, t=4)
                    )
                elif what[0] == "x":
                    load_x(int(what[1]))
                elif what[0] == "y":
                    load_y(0, int(what[1]))
                elif what == "w1":
                    nc.sync.dma_start(out=w1_sb[:], in_=W1g_words.rearrange("g p n -> p g n"))
                else:
                    for quad in range(4):
                        nc.sync.dma_start(
                            out=w1_sc[32 * quad : 32 * quad + 4, :, :].rearrange("r g n -> r (g n)").bitcast(I32).rearrange(
                                "r (g n) -> r g n", g=2
                            ),
                            in_=W1g_scales[:, 4 * quad : 4 * quad + 4, :].bitcast(I32).rearrange("g r n -> r g n"),
                        )
            for i in range(3, n_steps):
                load_x(i)
                for k in range(1, len(LATE)):
                    if max(LATE[k][2][0], 3) == i:
                        load_y(k, 0)
                        load_y(k, 1)
                if i == 8:
                    nc.sync.dma_start(out=b1_row[0:1, :], in_=b1g.unsqueeze(0))
                    nc.sync.dma_start(out=b2_sb[:], in_=b2g.partition_broadcast(P))
                    nc.sync.dma_start(out=w2_sb[:], in_=W2g_words[0])
                    for quad in range(4):
                        nc.sync.dma_start(
                            out=w2_sc[32 * quad : 32 * quad + 4, :].bitcast(I32),
                            in_=W2g_scales[0, 4 * quad : 4 * quad + 4, :].bitcast(I32),
                        )

            warm = small.tile([P, 1], F32, name="warm")
            nc.scalar.activation(out=warm[:], in_=ident[:, 0:1], func=RELU)

            x_bf = {}
            grouped = {}
            codes = {}
            scales = {}
            acc = {}
            issued = {}

            def mul(i):
                q, j0, n = steps[i]
                xs = stage.tile([P, widest * F], BF16, name="xs", align_bytes=64)
                x_bf[i] = xs
                wide = 1 if i <= DUP + AHEAD else 2
                piece = F // 2 if i == 0 and "s01" in HEAD else wide * F
                for c0 in range(0, n * F, piece):
                    w = min(piece, n * F - c0)
                    k0 = c0 % F
                    nc.vector.tensor_tensor(
                        out=xs[:, c0 : c0 + w],
                        in0=x_tiles[i][:, c0 : c0 + w].bitcast(FP8),
                        in1=scale_sb[:, k0 : k0 + w],
                        op=MULT,
                    )

            tile_no = [0]

            def turn(i):
                q, j0, n = steps[i]
                words = x_bf[i][:].bitcast(F32)
                gr = stage.tile([P, widest * F], BF16, name="gr", align_bytes=64)
                grouped[i] = gr
                for j in range(n):
                    tp = tr_ps.tile([P, 512], F32, name="tp", tag="tp")
                    for g in range(2):
                        for u in range(2):
                            w0 = j * 512 + 256 * g
                            k0 = (2 * g + u) * P
                            nc.tensor.transpose(tp[:, k0 : k0 + P], words[:, w0 + u : w0 + 256 : 2], ident[:])
                    out_words = gr[:, j * F : (j + 1) * F].bitcast(F32).rearrange("p (g r u) -> p g r u", g=2, u=2)
                    in_words = tp[:].rearrange("p (g u r) -> p g r u", g=2, u=2)
                    if tile_no[0] in XV:
                        nc.vector.tensor_copy(out=out_words, in_=in_words)
                    else:
                        nc.scalar.copy(out=out_words, in_=in_words)
                    tile_no[0] += 1

            def quantize(i):
                q, j0, n = steps[i]
                cd = stage.tile([P, widest * 256], U32, name="cd", align_bytes=64)
                sc = stage.tile([P, widest * 256], U8, name="sc", align_bytes=64)
                codes[i] = cd
                scales[i] = sc
                for a in range(0, n, 2):
                    b = min(n, a + 2)
                    nc.vector.quantize_mx(
                        out=cd[:, a * 256 : b * 256].bitcast(E4M3X4),
                        scales=sc[:, a * 256 : b * 256],
                        in_=grouped[i][:, a * F : b * F],
                    )

            def layer1(q, cd, sc, g):
                if q not in acc:
                    ac = acc_ps.tile([P, G], F32, name="ac")
                    acc[q] = ac
                    issued[q] = 0
                issued[q] += 1
                nc.tensor.matmul_mx(
                    out=acc[q][:],
                    lhsT=cd.bitcast(E4M3X4),
                    lhsT_scale=sc,
                    rhs=w1_sb[:, g, :].bitcast(E2M1X4),
                    rhs_scale=w1_sc[:, g, :],
                    start=(issued[q] == 1),
                    stop=(issued[q] == 2 * groups[q][3]),
                )

            def multiply(i):
                q, j0, n = steps[i]
                for j in range(n):
                    for g in range(2):
                        c0 = (2 * j + g) * P
                        layer1(q, codes[i][:, c0 : c0 + P], scales[i][:, c0 : c0 + P], g)

            yb = {}
            yp = {}
            yg = {}
            yc = {}

            def y_widen(k, half):
                if half == 0:
                    y_bf = late.tile([P, 4 * F], BF16, name="y_bf", align_bytes=64)
                    yb[k] = y_bf
                cols = slice(half * 2 * F, (half + 1) * 2 * F)
                if (k, half) in WV:
                    nc.vector.tensor_copy(out=yb[k][:, cols], in_=y_tiles[k][:, cols].bitcast(FP8))
                else:
                    nc.scalar.copy(out=yb[k][:, cols], in_=y_tiles[k][:, cols].bitcast(FP8))

            def y_turn(k, g, u):
                words = yb[k][:].bitcast(F32)
                if u == 0:
                    pairs = late.tile([P, 2, 512, 2], BF16, name="pairs", align_bytes=64)
                    yp[k, g] = pairs
                ty = ty_ps.tile([P, 512], F32, name="ty")
                for j in range(4):
                    w0 = j * 512 + 256 * g
                    nc.tensor.transpose(ty[:, j * P : (j + 1) * P], words[:, w0 + u : w0 + 256 : 2], ident[:])
                for e in range(2):
                    t = 2 * u + e
                    nc.scalar.activation(
                        out=yp[k, g][:, u, :, e],
                        in_=ty[:].bitcast(BF16).rearrange("p (r e) -> p r e", e=2)[:, :, e],
                        func=COPY,
                        scale=scale_kp[:, g, t : t + 1],
                    )

            def y_interleave(q, g):
                four = late.tile([P, 512, 4], BF16, name="four", align_bytes=64)
                yg[q, g] = four
                nc.vector.tensor_copy(
                    out=four[:].rearrange("p r k -> p (r k)").bitcast(F32).rearrange("p (r u) -> p r u", u=2),
                    in_=yp[q, g][:].rearrange("p u r e -> p (u r e)").bitcast(F32).rearrange("p (u r) -> p r u", u=2),
                )

            def y_quantize(q, g):
                ycd = late.tile([P, 512], U32, name="ycd", align_bytes=64)
                ysc = late.tile([P, 512], U8, name="ysc", align_bytes=64)
                yc[q, g] = (ycd, ysc)
                nc.vector.quantize_mx(
                    out=ycd[:].bitcast(E4M3X4),
                    scales=ysc[:],
                    in_=yg[q, g][:].rearrange("p r k -> p (r k)"),
                )

            def y_multiply(k, g):
                ycd, ysc = yc[k, g]
                for j in range(4):
                    layer1(LATE[k][0], ycd[:, j * P : (j + 1) * P], ysc[:, j * P : (j + 1) * P], g)

            fin = {}

            def fin_copy(q):
                y = small.tile([P, 4, P], F32, name="y", align_bytes=64)
                fin["y", q] = y
                nc.scalar.copy(out=y[:], in_=acc[q][:].rearrange("p (m t) -> p t m", t=4))

            def fin_sum(q):
                graphs = groups[q][0]
                pre = tr_ps.tile([P, 512], F32, name="pre", tag="tp")
                fin["pre", q] = pre
                for t in range(4):
                    cols = slice(t * graphs, (t + 1) * graphs)
                    nc.tensor.matmul(
                        pre[:, cols], lhsT=b1_row[:, t:G:4], rhs=ones64[:, 0:graphs], start=True, stop=False
                    )
                    nc.tensor.matmul(
                        pre[:, cols], lhsT=fin["y", q][:, t, :], rhs=members[graphs][:], start=False, stop=True
                    )

            def fin_relu(q):
                graphs = groups[q][0]
                reps = P // graphs
                m1 = small.tile([P, P, 4], BF16, name="m1", align_bytes=64)
                fin["m1", q] = m1
                sums = fin["pre", q][:, 0 : 4 * graphs].rearrange("p (t b) -> p b t", t=4)
                nc.scalar.activation(
                    out=m1[:].rearrange("p (b r) t -> p b r t", r=reps),
                    in_=sums.unsqueeze(2).to_broadcast([P, graphs, reps, 4]),
                    func=RELU,
                    scale=1.0 / NODES,
                )

            def fin_quantize(q):
                m1c = small.tile([P, P], U32, name="m1c", align_bytes=64)
                m1s = small.tile([P, P], U8, name="m1s", align_bytes=64)
                nc.vector.quantize_mx(
                    out=m1c[:].bitcast(E4M3X4),
                    scales=m1s[:],
                    in_=fin["m1", q][:].rearrange("p n t -> p (n t)"),
                )
                fin["m1q", q] = (m1c, m1s)

            def fin_multiply(q):
                o_ps = tr_ps.tile([P, 512], F32, name="o_ps", tag="tp")
                fin["o", q] = o_ps
                m1c, m1s = fin["m1q", q]
                nc.tensor.matmul_mx(
                    out=o_ps[:, 0:O],
                    lhsT=m1c[:].bitcast(E4M3X4),
                    lhsT_scale=m1s[:],
                    rhs=w2_sb[:].bitcast(E2M1X4),
                    rhs_scale=w2_sc[:],
                    start=True,
                    stop=True,
                )

            def fin_store(q):
                graphs, first, view, tiles = groups[q]
                tmp = small.tile([P, O], F32, name="tmp", align_bytes=64)
                nc.vector.tensor_tensor(out=tmp[:], in0=fin["o", q][:, 0:O], in1=b2_sb[:], op=ADD)
                reps = P // graphs
                nodes = NODES // reps
                dst = out[first : first + graphs].rearrange("b (r n) o -> (b r) (n o)", r=reps)
                if q == len(GROUPS) - 1 or OUT == 0:
                    o_sb = small.tile([P, 4, O], F32, name="o_sb", align_bytes=64)
                    nc.vector.tensor_scalar(
                        out=o_sb[:], in0=tmp[:].unsqueeze(1).to_broadcast([P, 4, O]), scalar1=0.0, scalar2=None, op0=MAX
                    )
                    nc.sync.dma_start(
                        out=dst.rearrange("p (k m) -> p k m", m=4 * O),
                        in_=o_sb[:].rearrange("p k o -> p (k o)").unsqueeze(1).to_broadcast([P, nodes // 4, 4 * O]),
                    )
                else:
                    o_row = small.tile([P, O], F32, name="o_row", align_bytes=64)
                    if OUT == 1:
                        nc.scalar.activation(out=o_row[:], in_=tmp[:], func=RELU)
                    else:
                        nc.vector.tensor_scalar(out=o_row[:], in0=tmp[:], scalar1=0.0, scalar2=None, op0=MAX)
                    nc.sync.dma_start(
                        out=dst.rearrange("p (k m) -> p k m", m=O),
                        in_=o_row[:].unsqueeze(1).to_broadcast([P, nodes, O]),
                    )

            todo = {}

            def at(step, where, fn, q):
                todo.setdefault((step, where), []).append((fn, q))

            def run(step, where):
                for fn, q in todo.get((step, where), []):
                    fn(q)

            for q in range(len(GROUPS) - 1):
                c = close[q]
                at(c + FIN[0], "mid", fin_copy, q)
                at(c + FIN[1], "sum", fin_sum, q)
                at(c + FIN[1], "mid", fin_relu, q)
                at(c + FIN[2], "mid", fin_quantize, q)
                at(c + FIN[3], "sum", fin_multiply, q)
                at(c + FIN[4], "end", fin_store, q)

            def late_items(i, first_stage, n_stages):
                return [
                    (k, s) for s in range(n_stages) for k in range(len(LATE)) if LATE[k][2][first_stage + s] == i
                ]

            def warm_up(k):
                if k < len(DUM) and DUM[k]:
                    du = tr_ps.tile([P, 512], F32, name="du", tag="tp")
                    for n in range(DUM[k]):
                        nc.tensor.matmul(du[:], lhsT=zero[:, 0:P], rhs=zero[:], start=True, stop=True)

            warm_up(0)
            for k, half in late_items(-1, 0, 2):
                y_widen(k, half)
            for i in range(AHEAD):
                mul(i)
            for i in range(TAHEAD):
                turn(i)
            for i in range(n_steps):
                for what in ORDER:
                    if what == "du":
                        warm_up(i + 1)
                    if what == "C":
                        for k, g in late_items(i, 6, 2):
                            y_interleave(k, g)
                    elif what == "mulA" and i + AHEAD < n_steps:
                        mul(i + AHEAD)
                    elif what == "W":
                        for k, half in late_items(i, 0, 2):
                            y_widen(k, half)
                    elif what == "E":
                        for k, gu in late_items(i, 2, 4):
                            y_turn(k, gu // 2, gu % 2)
                    elif what == "sum":
                        run(i, "sum")
                    elif what == "turnA" and i + TAHEAD < n_steps:
                        turn(i + TAHEAD)
                    elif what == "mid":
                        run(i, "mid")
                    elif what == "qz":
                        quantize(i)
                        if i == DUP:
                            nc.scalar.copy(out=scale_sb[:, F : 2 * F], in_=scale_sb[:, 0:F])
                    elif what == "qY":
                        for k, g in late_items(i, 6, 2):
                            y_quantize(k, g)
                    elif what == "mmA":
                        multiply(i)
                    elif what == "mmY":
                        for k, g in late_items(i, 6, 2):
                            y_multiply(k, g)
                    elif what == "end":
                        run(i, "end")
            for i in range(n_steps, n_steps + 10):
                for where in ("sum", "mid", "end"):
                    run(i, where)
            q = len(GROUPS) - 1
            fin_copy(q)
            fin_sum(q)
            fin_relu(q)
            fin_quantize(q)
            fin_multiply(q)
            fin_store(q)
